import numpy as np
import ml_dtypes


def mxq(x, axis, fmt="e4m3"):
    dtype, down = {"e4m3": (ml_dtypes.float8_e4m3fn, 7), "e5m2": (ml_dtypes.float8_e5m2, 14)}[fmt]
    v = np.moveaxis(np.asarray(x, np.float32).astype(ml_dtypes.bfloat16).astype(np.float64), axis, -1)
    blocks = v.reshape(v.shape[:-1] + (-1, 32))
    amax = np.abs(blocks).max(-1, keepdims=True)
    byte = np.maximum(np.where(amax > 0, np.frexp(amax)[1] - 1 + 127, 0) - down, 1)
    scale = np.exp2(byte - 127.0)
    codes = (blocks / scale).astype(np.float32).astype(dtype).astype(np.float64)
    return np.moveaxis((codes * scale).reshape(v.shape), -1, axis)


WIDE = False


def mx_kscale(k):
    if not WIDE:
        return np.ones(k)
    levels = np.array([10, -10, 5, -5, 0])
    a = np.random.permutation(np.resize(levels, k // 512 * 4)).reshape(k // 512, 4)
    idx = np.arange(k)
    return np.exp2(a[idx // 512, idx % 128 // 32])


BF16 = ml_dtypes.bfloat16


def bf(x):
    return np.asarray(x, np.float32).astype(BF16)


def f64(x):
    return np.asarray(x).astype(np.float64)


E2M1 = np.array([0.0, 0.5, 1.0, 1.5, 2.0, 3.0, 4.0, 6.0, -0.0, -0.5, -1.0, -1.5, -2.0, -3.0, -4.0, -6.0])


def pack_weight(w, fmt):
    k, n = w.shape
    w = f64(bf(w)).reshape(k // 32, 32, n)
    amax = np.abs(w).max(1)
    if fmt == "e4m3":
        byte = np.frexp(amax)[1] - 1 + 127 - 7
    else:
        mant, ex = np.frexp(amax / 6.0)
        byte = np.where(mant > 0.5, ex, ex - 1) + 127
    byte = np.clip(np.where(amax > 0, byte, 1), 1, 254)
    scaled = (w * np.exp2(127.0 - byte)[:, None, :]).reshape(k, n).astype(np.float32)
    by_word = np.ascontiguousarray(scaled.reshape(k // 512, 128, 4, n).transpose(0, 1, 3, 2))
    if fmt == "e4m3":
        words = by_word.astype(ml_dtypes.float8_e4m3fn).view(np.uint8)
    else:
        c = by_word.astype(ml_dtypes.float4_e2m1fn).view(np.uint8) & 0xF
        words = c[..., 0::2] | (c[..., 1::2] << 4)
    return np.ascontiguousarray(words), np.ascontiguousarray(byte.astype(np.uint8).reshape(k // 512, 16, n))


def unpack_weight(words, scales, fmt):
    g, p, n, _ = words.shape
    if fmt == "e4m3":
        vals = np.ascontiguousarray(words).view(ml_dtypes.float8_e4m3fn).astype(np.float64)
    else:
        nib = np.empty((g, p, n, 4), np.uint8)
        nib[..., 0::2] = words & 0xF
        nib[..., 1::2] = words >> 4
        vals = E2M1[nib]
    vals = vals * np.repeat(np.exp2(scales.astype(np.float64) - 127.0), 8, axis=1)[..., None]
    return vals.transpose(0, 1, 3, 2).reshape(g * 512, n)


B, S, I, Q = 4096, 3, 512, 512
LN_EPS = 1e-5


def setup_inputs():
    s = mx_kscale(I)
    language_features = bf(np.random.standard_normal((B, I)) * s)
    stack = np.random.standard_normal((S, I, Q)) / np.sqrt(I) / s[None, :, None]
    W_words, W_scales = pack_weight(stack.reshape(-1, Q), "e4m3")
    return {"language_features": language_features,
            "W_words": W_words,
            "W_scales": W_scales,
            "b": bf(np.random.standard_normal((S, Q)) * 0.2),
            "amplitude_weights": bf(np.random.standard_normal((S, Q))),
            "phase_weights": bf(np.random.standard_normal((S, Q))),
            "ln_gamma": bf(1.0 + 0.1 * np.random.standard_normal(Q)),
            "ln_beta": bf(0.1 * np.random.standard_normal(Q))}


def reference(language_features, W_words, W_scales, b, amplitude_weights, phase_weights, ln_gamma, ln_beta):
    xq = mxq(f64(language_features), 1, "e4m3")
    wq = unpack_weight(W_words, W_scales, "e4m3").reshape(S, I, Q)
    states = (xq @ wq).transpose(1, 0, 2) + f64(b)[None, :, :]
    a = f64(amplitude_weights)
    e = np.exp(a - a.max(axis=0, keepdims=True))
    amplitudes = e / e.sum(axis=0, keepdims=True)
    mix = amplitudes * np.cos(f64(phase_weights))
    sup = states * mix[None, :, :]
    mean = sup.mean(axis=-1, keepdims=True)
    var = sup.var(axis=-1, keepdims=True)
    return (sup - mean) * (1.0 / np.sqrt(var + LN_EPS)) * f64(ln_gamma) + f64(ln_beta)

@@ -1,0 +1,309 @@
+import math
+from contextlib import ExitStack
+
+import concourse.mybir as mybir
+from concourse.masks import make_identity
+
+F32 = mybir.dt.float32
+BF16 = mybir.dt.bfloat16
+I32 = mybir.dt.int32
+U32 = mybir.dt.uint32
+U8 = mybir.dt.uint8
+FP8X4 = mybir.dt.float8_e4m3fn_x4
+ALU = mybir.AluOpType
+ACT = mybir.ActivationFunctionType
+
+P = 128
+ROWS = 4096
+K = 512
+STATES = 3
+N = 512
+LN_EPS = 1e-5
+
+BLOCK_ROWS = 512
+BLOCKS = ROWS // BLOCK_ROWS
+ROW_TILES = BLOCK_ROWS // P
+N_CHUNKS = N // P
+K_WORDS = K // 2
+GROUPS = BLOCKS * STATES
+TILES = GROUPS * ROW_TILES
+ROUND_MAGIC = 1.5 * 2.0**23
+
+FLOPS = 2 * ROWS * K * STATES * N
+
+
+def tile_quantumsuperposition_t_e_kernel(
+    tc,
+    language_features,
+    W_words,
+    W_scales,
+    b,
+    amplitude_weights,
+    phase_weights,
+    ln_gamma,
+    ln_beta,
+    out,
+):
+    nc = tc.nc
+    x_blocks = language_features.rearrange("(blk p t) k -> blk p t k", p=P, t=ROW_TILES)
+    out_groups = out.rearrange("(blk p t) s n -> blk s p t n", p=P, t=ROW_TILES)
+
+    with ExitStack() as ctx:
+        ctx.enter_context(tc.manual_schedule())
+        const = ctx.enter_context(tc.tile_pool(name="const", bufs=1))
+        small = ctx.enter_context(tc.tile_pool(name="small", bufs=1))
+
+        param_rows = const.tile([P, P], BF16)
+        nc.vector.memset(param_rows[:], 0.0)
+        for place, param in enumerate((amplitude_weights, phase_weights, b)):
+            first = place * STATES * N_CHUNKS
+            nc.sync.dma_start(
+                out=param_rows[first : first + STATES * N_CHUNKS, :],
+                in_=param.rearrange("s (j p) -> (s j) p", p=P),
+            )
+
+        x_pool = ctx.enter_context(tc.tile_pool(name="x_pool", bufs=BLOCKS))
+        x_tiles = []
+
+        def load_x(blk):
+            x_rows = x_pool.tile([P, ROW_TILES, K], BF16)
+            nc.sync.dma_start(out=x_rows[:], in_=x_blocks[blk])
+            x_tiles.append(x_rows)
+
+        load_x(0)
+        load_x(1)
+
+        w_scales = const.tile([P, STATES, N], U8, align_bytes=64)
+        nc.vector.memset(w_scales[:].bitcast(I32), 0)
+        for quad in range(4):
+            nc.sync.dma_start(
+                out=w_scales[32 * quad : 32 * quad + 4, :, :].bitcast(I32),
+                in_=W_scales[:, 4 * quad : 4 * quad + 4, :].rearrange("g r n -> r g n").bitcast(I32),
+            )
+        w_codes = const.tile([P, STATES, N], U32, align_bytes=64)
+        nc.sync.dma_start(
+            out=w_codes[:].bitcast(I32),
+            in_=W_words.rearrange("g p n t -> p g (n t)").bitcast(I32),
+        )
+        for blk in range(2, BLOCKS):
+            load_x(blk)
+
+        gamma_bf = const.tile([P, N], BF16)
+        beta_bf = const.tile([P, N], BF16)
+        nc.sync.dma_start(out=gamma_bf[:], in_=ln_gamma.partition_broadcast(P))
+        nc.sync.dma_start(out=beta_bf[:], in_=ln_beta.partition_broadcast(P))
+
+        ident_bf = const.tile([P, P], BF16)
+        make_identity(nc, ident_bf[:])
+        ident_f32 = const.tile([P, P], F32)
+        make_identity(nc, ident_f32[:])
+        eps = const.tile([P, 1], F32)
+        nc.vector.memset(eps[:], LN_EPS)
+
+        x_codes = const.tile([P, BLOCKS, BLOCK_ROWS], U32, align_bytes=64)
+        x_scales = const.tile([P, BLOCKS, BLOCK_ROWS], U8, align_bytes=64)
+        mix_col = const.tile([P, STATES, N_CHUNKS], F32)
+        shift_col = const.tile([P, STATES, N_CHUNKS], F32)
+        by_state = [P, STATES, N_CHUNKS]
+
+        with ExitStack() as head:
+            head_psum = head.enter_context(tc.psum_pool(name="head_psum", bufs=4))
+            grouped_pool = head.enter_context(tc.tile_pool(name="grouped_pool", bufs=3))
+
+            param_ps = head_psum.tile([P, P], BF16, bufs=1)
+            nc.tensor.transpose(param_ps[:], param_rows[:], ident_bf[:])
+            params = small.tile([P, 3, STATES, N_CHUNKS], F32)
+            nc.vector.tensor_copy(
+                out=params[:].rearrange("p a s j -> p (a s j)"),
+                in_=param_ps[:, 0 : 3 * STATES * N_CHUNKS],
+            )
+            amplitude = params[:, 0, :, :]
+            phase = params[:, 1, :, :]
+            bias = params[:, 2, :, :]
+
+            peak = small.tile([P, N_CHUNKS], F32)
+            nc.vector.tensor_max(out=peak[:], in0=amplitude[:, 0, :], in1=amplitude[:, 1, :])
+            nc.vector.tensor_max(out=peak[:], in0=peak[:], in1=amplitude[:, 2, :])
+            expo = small.tile(by_state, F32)
+            nc.vector.tensor_tensor(
+                out=expo[:],
+                in0=amplitude,
+                in1=peak[:].unsqueeze(1).to_broadcast(by_state),
+                op=ALU.subtract,
+            )
+            nc.scalar.activation(out=expo[:], in_=expo[:], func=ACT.Exp)
+
+            turns = small.tile(by_state, F32)
+            nc.vector.tensor_scalar(
+                out=turns[:], in0=phase, scalar1=1.0 / (2.0 * math.pi), scalar2=None, op0=ALU.mult
+            )
+            whole = small.tile(by_state, F32)
+            nc.vector.tensor_scalar(
+                out=whole[:], in0=turns[:], scalar1=ROUND_MAGIC, scalar2=None, op0=ALU.add
+            )
+            nc.vector.tensor_scalar(
+                out=whole[:], in0=whole[:], scalar1=ROUND_MAGIC, scalar2=None, op0=ALU.subtract
+            )
+            half_sin = small.tile(by_state, F32)
+            nc.vector.tensor_tensor(out=half_sin[:], in0=turns[:], in1=whole[:], op=ALU.subtract)
+            nc.scalar.activation(out=half_sin[:], in_=half_sin[:], func=ACT.Sin, scale=math.pi)
+
+            grouped_tiles = []
+
+            def transpose_block(blk):
+                grouped = grouped_pool.tile([P, 4 * BLOCK_ROWS], BF16, align_bytes=64)
+                grouped_words = grouped[:].bitcast(F32).rearrange(
+                    "q (t r u) -> q t r u", t=ROW_TILES, u=2
+                )
+                x_words = x_tiles[blk][:].bitcast(F32)
+                for half, copy_out in enumerate((nc.vector.tensor_copy, nc.scalar.copy)):
+                    x_t = head_psum.tile([P, 2, 2, P], F32)
+                    for t in range(2):
+                        for u in range(2):
+                            nc.tensor.transpose(
+                                x_t[:, t, u, :], x_words[:, 2 * half + t, u:K_WORDS:2], ident_f32[:]
+                            )
+                    copy_out(
+                        out=grouped_words[:, 2 * half : 2 * half + 2, :, :],
+                        in_=x_t[:].rearrange("q t u r -> q t r u"),
+                    )
+                grouped_tiles.append(grouped)
+
+            def quantise_block(blk):
+                nc.vector.quantize_mx(
+                    out=x_codes[:, blk, :].bitcast(FP8X4),
+                    scales=x_scales[:, blk, :],
+                    in_=grouped_tiles[blk][:],
+                )
+
+            transpose_block(0)
+            for blk in range(1, BLOCKS):
+                transpose_block(blk)
+                quantise_block(blk - 1)
+            quantise_block(BLOCKS - 1)
+
+            total = small.tile([P, N_CHUNKS], F32)
+            nc.vector.tensor_add(out=total[:], in0=expo[:, 0, :], in1=expo[:, 1, :])
+            nc.vector.tensor_add(out=total[:], in0=total[:], in1=expo[:, 2, :])
+            nc.vector.reciprocal(out=total[:], in_=total[:])
+            cosine = small.tile(by_state, F32)
+            nc.vector.tensor_mul(out=cosine[:], in0=half_sin[:], in1=half_sin[:])
+            nc.vector.tensor_scalar(
+                out=cosine[:], in0=cosine[:], scalar1=-2.0, scalar2=1.0, op0=ALU.mult, op1=ALU.add
+            )
+            nc.vector.tensor_mul(
+                out=mix_col[:], in0=expo[:], in1=total[:].unsqueeze(1).to_broadcast(by_state)
+            )
+            nc.vector.tensor_mul(out=mix_col[:], in0=mix_col[:], in1=cosine[:])
+            nc.vector.tensor_mul(out=shift_col[:], in0=bias, in1=mix_col[:])
+
+            gamma_row = const.tile([P, N], F32)
+            beta_row = const.tile([P, N], F32)
+            nc.vector.tensor_copy(out=gamma_row[:], in_=gamma_bf[:])
+            nc.vector.tensor_copy(out=beta_row[:], in_=beta_bf[:])
+
+        y_psum = ctx.enter_context(tc.psum_pool(name="y_psum", bufs=N_CHUNKS))
+        sup_psum = ctx.enter_context(tc.psum_pool(name="sup_psum", bufs=4))
+        sup_t_pool = ctx.enter_context(tc.tile_pool(name="sup_t_pool", bufs=3))
+        stat_pool = ctx.enter_context(tc.tile_pool(name="stat_pool", bufs=4))
+        out_pool = ctx.enter_context(tc.tile_pool(name="out_pool", bufs=5))
+        sup_t_of = {}
+        sup_of = {}
+        halves_of = {}
+        mean_var_of = {}
+        rstd_of = {}
+        out_of = {}
+
+        def start_group(g):
+            blk, s = divmod(g, STATES)
+            sup_t = sup_t_pool.tile([P, N_CHUNKS, BLOCK_ROWS], F32)
+            banks = []
+            for j in range(N_CHUNKS):
+                cols = slice(j * P, (j + 1) * P)
+                y_t = y_psum.tile([P, BLOCK_ROWS], F32)
+                nc.tensor.matmul_mx(
+                    out=y_t[:],
+                    lhsT=w_codes[:, s, cols].bitcast(FP8X4),
+                    lhsT_scale=w_scales[:, s, cols],
+                    rhs=x_codes[:, blk, :].bitcast(FP8X4),
+                    rhs_scale=x_scales[:, blk, :],
+                    start=True,
+                    stop=True,
+                )
+                banks.append(y_t)
+            for j in range(N_CHUNKS):
+                nc.scalar.activation(
+                    out=sup_t[:, j, :],
+                    in_=banks[j][:],
+                    func=ACT.Identity,
+                    scale=mix_col[:, s, j : j + 1],
+                    bias=shift_col[:, s, j : j + 1],
+                )
+            sup_t_of[g] = sup_t
+            mean_var = stat_pool.tile([P, ROW_TILES, 2], F32)
+            mean_var_of[g] = mean_var
+            out_tile = out_pool.tile([P, ROW_TILES, N], F32)
+            out_of[g] = out_tile
+
+        def transpose_tile(i):
+            g, t = divmod(i, ROW_TILES)
+            sup = sup_psum.tile([P, N], F32)
+            for j in range(N_CHUNKS):
+                nc.tensor.transpose(
+                    sup[:, j * P : (j + 1) * P], sup_t_of[g][:, j, t * P : (t + 1) * P], ident_f32[:]
+                )
+            sup_of[i] = sup
+
+        def row_sums(i):
+            halves = stat_pool.tile([P, 6], F32)
+            nc.vector.bn_stats(out=halves[:], in_=sup_of[i][:])
+            halves_of[i] = halves
+
+        def mean_and_variance(i):
+            g, t = divmod(i, ROW_TILES)
+            nc.vector.bn_aggr(out=mean_var_of[g][:, t, :], in_=halves_of[i][:])
+
+        def centre_times_gamma(i):
+            g, t = divmod(i, ROW_TILES)
+            nc.vector.scalar_tensor_tensor(
+                out=out_of[g][:, t, :],
+                in0=sup_of[i][:],
+                scalar=mean_var_of[g][:, t, 0:1],
+                in1=gamma_row[:],
+                op0=ALU.subtract,
+                op1=ALU.mult,
+            )
+
+        def inverse_deviation(g):
+            rstd = stat_pool.tile([P, ROW_TILES], F32)
+            nc.scalar.activation(
+                out=rstd[:], in_=mean_var_of[g][:, :, 1], func=ACT.Sqrt, bias=eps[:, 0:1], scale=1.0
+            )
+            nc.vector.reciprocal(out=rstd[:], in_=rstd[:])
+            rstd_of[g] = rstd
+
+        def finish_group(g):
+            blk, s = divmod(g, STATES)
+            for t in range(ROW_TILES):
+                rows = out_of[g][:, t, :]
+                nc.scalar.activation(
+                    out=rows, in_=rows, func=ACT.Identity, scale=rstd_of[g][:, t : t + 1]
+                )
+                nc.gpsimd.tensor_tensor(out=rows, in0=rows, in1=beta_row[:], op=ALU.add)
+            nc.sync.dma_start(out=out_groups[blk, s], in_=out_of[g][:])
+
+        for g in range(-1, GROUPS + 2):
+            if g + 1 < GROUPS:
+                start_group(g + 1)
+            for i in range(g * ROW_TILES, (g + 1) * ROW_TILES):
+                if 0 <= i < TILES:
+                    transpose_tile(i)
+                    row_sums(i)
+                if 0 <= i - 1 < TILES:
+                    mean_and_variance(i - 1)
+                if 0 <= i - 2 < TILES:
+                    centre_times_gamma(i - 2)
+            if 0 <= g - 1 < GROUPS:
+                inverse_deviation(g - 1)
+            if 0 <= g - 2 < GROUPS:
+                finish_group(g - 2)

@@ -29,6 +29,12 @@ GROUPS = BLOCKS * STATES
 TILES = GROUPS * ROW_TILES
 ROUND_MAGIC = 1.5 * 2.0**23
 
+Y_BANKS = 2
+SUP_BANKS = 6
+TRANSPOSE_AHEAD = SUP_BANKS - 3
+MIX_AHEAD = TRANSPOSE_AHEAD + N_CHUNKS + 1
+FINISH_BEHIND = ROW_TILES + 2
+
 FLOPS = 2 * ROWS * K * STATES * N
 
 
@@ -202,9 +208,9 @@ def tile_quantumsuperposition_t_e_kernel(
             nc.vector.tensor_copy(out=gamma_row[:], in_=gamma_bf[:])
             nc.vector.tensor_copy(out=beta_row[:], in_=beta_bf[:])
 
-        y_psum = ctx.enter_context(tc.psum_pool(name="y_psum", bufs=N_CHUNKS))
-        sup_psum = ctx.enter_context(tc.psum_pool(name="sup_psum", bufs=4))
-        sup_t_pool = ctx.enter_context(tc.tile_pool(name="sup_t_pool", bufs=3))
+        y_psum = ctx.enter_context(tc.psum_pool(name="y_psum", bufs=Y_BANKS))
+        sup_psum = ctx.enter_context(tc.psum_pool(name="sup_psum", bufs=SUP_BANKS))
+        sup_t_pool = ctx.enter_context(tc.tile_pool(name="sup_t_pool", bufs=4))
         stat_pool = ctx.enter_context(tc.tile_pool(name="stat_pool", bufs=4))
         out_pool = ctx.enter_context(tc.tile_pool(name="out_pool", bufs=5))
         sup_t_of = {}
@@ -214,36 +220,30 @@ def tile_quantumsuperposition_t_e_kernel(
         rstd_of = {}
         out_of = {}
 
-        def start_group(g):
+        def multiply_and_mix(c):
+            g, j = divmod(c, N_CHUNKS)
             blk, s = divmod(g, STATES)
-            sup_t = sup_t_pool.tile([P, N_CHUNKS, BLOCK_ROWS], F32)
-            banks = []
-            for j in range(N_CHUNKS):
-                cols = slice(j * P, (j + 1) * P)
-                y_t = y_psum.tile([P, BLOCK_ROWS], F32)
-                nc.tensor.matmul_mx(
-                    out=y_t[:],
-                    lhsT=w_codes[:, s, cols].bitcast(FP8X4),
-                    lhsT_scale=w_scales[:, s, cols],
-                    rhs=x_codes[:, blk, :].bitcast(FP8X4),
-                    rhs_scale=x_scales[:, blk, :],
-                    start=True,
-                    stop=True,
-                )
-                banks.append(y_t)
-            for j in range(N_CHUNKS):
-                nc.scalar.activation(
-                    out=sup_t[:, j, :],
-                    in_=banks[j][:],
-                    func=ACT.Identity,
-                    scale=mix_col[:, s, j : j + 1],
-                    bias=shift_col[:, s, j : j + 1],
-                )
-            sup_t_of[g] = sup_t
-            mean_var = stat_pool.tile([P, ROW_TILES, 2], F32)
-            mean_var_of[g] = mean_var
-            out_tile = out_pool.tile([P, ROW_TILES, N], F32)
-            out_of[g] = out_tile
+            if j == 0:
+                sup_t = sup_t_pool.tile([P, N_CHUNKS, BLOCK_ROWS], F32)
+                sup_t_of[g] = sup_t
+            cols = slice(j * P, (j + 1) * P)
+            y_t = y_psum.tile([P, BLOCK_ROWS], F32)
+            nc.tensor.matmul_mx(
+                out=y_t[:],
+                lhsT=w_codes[:, s, cols].bitcast(FP8X4),
+                lhsT_scale=w_scales[:, s, cols],
+                rhs=x_codes[:, blk, :].bitcast(FP8X4),
+                rhs_scale=x_scales[:, blk, :],
+                start=True,
+                stop=True,
+            )
+            nc.scalar.activation(
+                out=sup_t_of[g][:, j, :],
+                in_=y_t[:],
+                func=ACT.Identity,
+                scale=mix_col[:, s, j : j + 1],
+                bias=shift_col[:, s, j : j + 1],
+            )
 
         def transpose_tile(i):
             g, t = divmod(i, ROW_TILES)
@@ -261,10 +261,22 @@ def tile_quantumsuperposition_t_e_kernel(
 
         def mean_and_variance(i):
             g, t = divmod(i, ROW_TILES)
+            if t == 0:
+                mean_var = stat_pool.tile([P, ROW_TILES, 2], F32)
+                mean_var_of[g] = mean_var
             nc.vector.bn_aggr(out=mean_var_of[g][:, t, :], in_=halves_of[i][:])
+            if t == ROW_TILES - 1:
+                rstd = stat_pool.tile([P, ROW_TILES], F32)
+                nc.scalar.activation(
+                    out=rstd[:], in_=mean_var_of[g][:, :, 1], func=ACT.Sqrt, bias=eps[:, 0:1], scale=1.0
+                )
+                rstd_of[g] = rstd
 
         def centre_times_gamma(i):
             g, t = divmod(i, ROW_TILES)
+            if t == 0:
+                out_tile = out_pool.tile([P, ROW_TILES, N], F32)
+                out_of[g] = out_tile
             nc.vector.scalar_tensor_tensor(
                 out=out_of[g][:, t, :],
                 in0=sup_of[i][:],
@@ -273,37 +285,28 @@ def tile_quantumsuperposition_t_e_kernel(
                 op0=ALU.subtract,
                 op1=ALU.mult,
             )
+            if t == ROW_TILES - 1:
+                nc.vector.reciprocal(out=rstd_of[g][:], in_=rstd_of[g][:])
 
-        def inverse_deviation(g):
-            rstd = stat_pool.tile([P, ROW_TILES], F32)
-            nc.scalar.activation(
-                out=rstd[:], in_=mean_var_of[g][:, :, 1], func=ACT.Sqrt, bias=eps[:, 0:1], scale=1.0
-            )
-            nc.vector.reciprocal(out=rstd[:], in_=rstd[:])
-            rstd_of[g] = rstd
-
-        def finish_group(g):
+        def finish_tile(i):
+            g, t = divmod(i, ROW_TILES)
             blk, s = divmod(g, STATES)
-            for t in range(ROW_TILES):
-                rows = out_of[g][:, t, :]
-                nc.scalar.activation(
-                    out=rows, in_=rows, func=ACT.Identity, scale=rstd_of[g][:, t : t + 1]
-                )
-                nc.gpsimd.tensor_tensor(out=rows, in0=rows, in1=beta_row[:], op=ALU.add)
-            nc.sync.dma_start(out=out_groups[blk, s], in_=out_of[g][:])
+            rows = out_of[g][:, t, :]
+            nc.scalar.activation(out=rows, in_=rows, func=ACT.Identity, scale=rstd_of[g][:, t : t + 1])
+            nc.gpsimd.tensor_tensor(out=rows, in0=rows, in1=beta_row[:], op=ALU.add)
+            if t == ROW_TILES - 1:
+                nc.sync.dma_start(out=out_groups[blk, s], in_=out_of[g][:])
 
-        for g in range(-1, GROUPS + 2):
-            if g + 1 < GROUPS:
-                start_group(g + 1)
-            for i in range(g * ROW_TILES, (g + 1) * ROW_TILES):
-                if 0 <= i < TILES:
-                    transpose_tile(i)
-                    row_sums(i)
-                if 0 <= i - 1 < TILES:
-                    mean_and_variance(i - 1)
-                if 0 <= i - 2 < TILES:
-                    centre_times_gamma(i - 2)
-            if 0 <= g - 1 < GROUPS:
-                inverse_deviation(g - 1)
-            if 0 <= g - 2 < GROUPS:
-                finish_group(g - 2)
+        for i in range(-MIX_AHEAD, TILES + FINISH_BEHIND):
+            if i + MIX_AHEAD < TILES:
+                multiply_and_mix(i + MIX_AHEAD)
+            if 0 <= i + TRANSPOSE_AHEAD < TILES:
+                transpose_tile(i + TRANSPOSE_AHEAD)
+            if 0 <= i < TILES:
+                row_sums(i)
+            if 0 <= i - 1 < TILES:
+                mean_and_variance(i - 1)
+            if 0 <= i - 2 < TILES:
+                centre_times_gamma(i - 2)
+            if 0 <= i - FINISH_BEHIND:
+                finish_tile(i - FINISH_BEHIND)

@@ -68,6 +68,11 @@ def tile_quantumsuperposition_t_e_kernel(
                 in_=param.rearrange("s (j p) -> (s j) p", p=P),
             )
 
+        norm_rows = const.tile([P, 2, N], BF16)
+        nc.vector.memset(norm_rows[:], 0.0)
+        nc.sync.dma_start(out=norm_rows[0:1, 0, :], in_=ln_gamma.unsqueeze(0))
+        nc.sync.dma_start(out=norm_rows[0:1, 1, :], in_=ln_beta.unsqueeze(0))
+
         x_pool = ctx.enter_context(tc.tile_pool(name="x_pool", bufs=BLOCKS))
         x_tiles = []
 
@@ -94,15 +99,12 @@ def tile_quantumsuperposition_t_e_kernel(
         for blk in range(2, BLOCKS):
             load_x(blk)
 
-        gamma_bf = const.tile([P, N], BF16)
-        beta_bf = const.tile([P, N], BF16)
-        nc.sync.dma_start(out=gamma_bf[:], in_=ln_gamma.partition_broadcast(P))
-        nc.sync.dma_start(out=beta_bf[:], in_=ln_beta.partition_broadcast(P))
-
         ident_bf = const.tile([P, P], BF16)
         make_identity(nc, ident_bf[:])
         ident_f32 = const.tile([P, P], F32)
         make_identity(nc, ident_f32[:])
+        ones = const.tile([P, P], BF16)
+        nc.vector.memset(ones[:], 1.0)
         eps = const.tile([P, 1], F32)
         nc.vector.memset(eps[:], LN_EPS)
 
@@ -123,6 +125,15 @@ def tile_quantumsuperposition_t_e_kernel(
                 out=params[:].rearrange("p a s j -> p (a s j)"),
                 in_=param_ps[:, 0 : 3 * STATES * N_CHUNKS],
             )
+            gamma_row = const.tile([P, N], F32)
+            beta_row = const.tile([P, N], F32)
+            for place, spread in enumerate((gamma_row, beta_row)):
+                spread_ps = head_psum.tile([P, N], F32, bufs=2)
+                nc.tensor.matmul(
+                    out=spread_ps[:], lhsT=ones[:], rhs=norm_rows[:, place, :], start=True, stop=True
+                )
+                nc.scalar.copy(out=spread[:], in_=spread_ps[:])
+
             amplitude = params[:, 0, :, :]
             phase = params[:, 1, :, :]
             bias = params[:, 2, :, :]
@@ -186,7 +197,6 @@ def tile_quantumsuperposition_t_e_kernel(
             for blk in range(1, BLOCKS):
                 transpose_block(blk)
                 quantise_block(blk - 1)
-            quantise_block(BLOCKS - 1)
 
             total = small.tile([P, N_CHUNKS], F32)
             nc.vector.tensor_add(out=total[:], in0=expo[:, 0, :], in1=expo[:, 1, :])
@@ -203,10 +213,7 @@ def tile_quantumsuperposition_t_e_kernel(
             nc.vector.tensor_mul(out=mix_col[:], in0=mix_col[:], in1=cosine[:])
             nc.vector.tensor_mul(out=shift_col[:], in0=bias, in1=mix_col[:])
 
-            gamma_row = const.tile([P, N], F32)
-            beta_row = const.tile([P, N], F32)
-            nc.vector.tensor_copy(out=gamma_row[:], in_=gamma_bf[:])
-            nc.vector.tensor_copy(out=beta_row[:], in_=beta_bf[:])
+            quantise_block(BLOCKS - 1)
 
         y_psum = ctx.enter_context(tc.psum_pool(name="y_psum", bufs=Y_BANKS))
         sup_psum = ctx.enter_context(tc.psum_pool(name="sup_psum", bufs=SUP_BANKS))
@@ -292,10 +299,28 @@ def tile_quantumsuperposition_t_e_kernel(
             g, t = divmod(i, ROW_TILES)
             blk, s = divmod(g, STATES)
             rows = out_of[g][:, t, :]
-            nc.scalar.activation(out=rows, in_=rows, func=ACT.Identity, scale=rstd_of[g][:, t : t + 1])
-            nc.gpsimd.tensor_tensor(out=rows, in0=rows, in1=beta_row[:], op=ALU.add)
-            if t == ROW_TILES - 1:
-                nc.sync.dma_start(out=out_groups[blk, s], in_=out_of[g][:])
+            if g < GROUPS - 1:
+                nc.scalar.activation(
+                    out=rows, in_=rows, func=ACT.Identity, scale=rstd_of[g][:, t : t + 1]
+                )
+                if t == ROW_TILES - 1:
+                    nc.gpsimd.tensor_tensor(
+                        out=out_of[g][:],
+                        in0=out_of[g][:],
+                        in1=beta_row[:].unsqueeze(1).to_broadcast([P, ROW_TILES, N]),
+                        op=ALU.add,
+                    )
+                    nc.sync.dma_start(out=out_groups[blk, s], in_=out_of[g][:])
+            else:
+                nc.vector.scalar_tensor_tensor(
+                    out=rows,
+                    in0=rows,
+                    scalar=rstd_of[g][:, t : t + 1],
+                    in1=beta_row[:],
+                    op0=ALU.mult,
+                    op1=ALU.add,
+                )
+                nc.sync.dma_start(out=out_groups[blk, s][:, t, :], in_=rows)
 
         for i in range(-MIX_AHEAD, TILES + FINISH_BEHIND):
             if i + MIX_AHEAD < TILES:

@@ -33,7 +33,9 @@ Y_BANKS = 2
 SUP_BANKS = 6
 TRANSPOSE_AHEAD = SUP_BANKS - 3
 MIX_AHEAD = TRANSPOSE_AHEAD + N_CHUNKS + 1
-FINISH_BEHIND = ROW_TILES + 2
+FINISH_BEHIND = ROW_TILES + 1
+VECTOR_GROUPS = 3
+GPSIMD_TILES = (GROUPS - VECTOR_GROUPS) * ROW_TILES
 
 FLOPS = 2 * ROWS * K * STATES * N
 
@@ -164,6 +166,8 @@ def tile_quantumsuperposition_t_e_kernel(
             half_sin = small.tile(by_state, F32)
             nc.vector.tensor_tensor(out=half_sin[:], in0=turns[:], in1=whole[:], op=ALU.subtract)
             nc.scalar.activation(out=half_sin[:], in_=half_sin[:], func=ACT.Sin, scale=math.pi)
+            warm = small.tile([P, 1], F32)
+            nc.scalar.activation(out=warm[:], in_=eps[:], func=ACT.Abs_reciprocal_sqrt)
 
             grouped_tiles = []
 
@@ -275,7 +279,11 @@ def tile_quantumsuperposition_t_e_kernel(
             if t == ROW_TILES - 1:
                 rstd = stat_pool.tile([P, ROW_TILES], F32)
                 nc.scalar.activation(
-                    out=rstd[:], in_=mean_var_of[g][:, :, 1], func=ACT.Sqrt, bias=eps[:, 0:1], scale=1.0
+                    out=rstd[:],
+                    in_=mean_var_of[g][:, :, 1],
+                    func=ACT.Abs_reciprocal_sqrt,
+                    bias=eps[:, 0:1],
+                    scale=1.0,
                 )
                 rstd_of[g] = rstd
 
@@ -292,37 +300,36 @@ def tile_quantumsuperposition_t_e_kernel(
                 op0=ALU.subtract,
                 op1=ALU.mult,
             )
-            if t == ROW_TILES - 1:
-                nc.vector.reciprocal(out=rstd_of[g][:], in_=rstd_of[g][:])
 
         def finish_tile(i):
             g, t = divmod(i, ROW_TILES)
             blk, s = divmod(g, STATES)
             rows = out_of[g][:, t, :]
-            if g < GROUPS - 1:
-                nc.scalar.activation(
-                    out=rows, in_=rows, func=ACT.Identity, scale=rstd_of[g][:, t : t + 1]
+            nc.scalar.activation(out=rows, in_=rows, func=ACT.Identity, scale=rstd_of[g][:, t : t + 1])
+            if t == ROW_TILES - 1:
+                nc.gpsimd.tensor_tensor(
+                    out=out_of[g][:],
+                    in0=out_of[g][:],
+                    in1=beta_row[:].unsqueeze(1).to_broadcast([P, ROW_TILES, N]),
+                    op=ALU.add,
                 )
-                if t == ROW_TILES - 1:
-                    nc.gpsimd.tensor_tensor(
-                        out=out_of[g][:],
-                        in0=out_of[g][:],
-                        in1=beta_row[:].unsqueeze(1).to_broadcast([P, ROW_TILES, N]),
-                        op=ALU.add,
-                    )
-                    nc.sync.dma_start(out=out_groups[blk, s], in_=out_of[g][:])
-            else:
-                nc.vector.scalar_tensor_tensor(
-                    out=rows,
-                    in0=rows,
-                    scalar=rstd_of[g][:, t : t + 1],
-                    in1=beta_row[:],
-                    op0=ALU.mult,
-                    op1=ALU.add,
-                )
-                nc.sync.dma_start(out=out_groups[blk, s][:, t, :], in_=rows)
+                nc.sync.dma_start(out=out_groups[blk, s], in_=out_of[g][:])
 
-        for i in range(-MIX_AHEAD, TILES + FINISH_BEHIND):
+        def finish_tile_on_vector(i, beta_bank):
+            g, t = divmod(i, ROW_TILES)
+            blk, s = divmod(g, STATES)
+            rows = out_of[g][:, t, :]
+            nc.vector.scalar_tensor_tensor(
+                out=rows,
+                in0=rows,
+                scalar=rstd_of[g][:, t : t + 1],
+                in1=beta_bank[:],
+                op0=ALU.mult,
+                op1=ALU.add,
+            )
+            nc.sync.dma_start(out=out_groups[blk, s][:, t, :], in_=rows)
+
+        for i in range(-MIX_AHEAD, TILES + 2):
             if i + MIX_AHEAD < TILES:
                 multiply_and_mix(i + MIX_AHEAD)
             if 0 <= i + TRANSPOSE_AHEAD < TILES:
@@ -333,5 +340,10 @@ def tile_quantumsuperposition_t_e_kernel(
                 mean_and_variance(i - 1)
             if 0 <= i - 2 < TILES:
                 centre_times_gamma(i - 2)
-            if 0 <= i - FINISH_BEHIND:
+            if 0 <= i - FINISH_BEHIND < GPSIMD_TILES:
                 finish_tile(i - FINISH_BEHIND)
+
+        beta_bank = sup_psum.tile([P, N], F32, tag="sup")
+        nc.tensor.matmul(out=beta_bank[:], lhsT=ones[:], rhs=norm_rows[:, 1, :], start=True, stop=True)
+        for i in range(GPSIMD_TILES, TILES):
+            finish_tile_on_vector(i, beta_bank)

@@ -20,6 +20,9 @@ STATES = 3
 N = 512
 LN_EPS = 1e-5
 
+PACK = 4
+QUADRANTS = 4
+LIVE_ROWS = 4
 BLOCK_ROWS = 512
 BLOCKS = ROWS // BLOCK_ROWS
 ROW_TILES = BLOCK_ROWS // P
@@ -27,6 +30,7 @@ N_CHUNKS = N // P
 K_WORDS = K // 2
 GROUPS = BLOCKS * STATES
 TILES = GROUPS * ROW_TILES
+BN_STATS_DIM = 6
 ROUND_MAGIC = 1.5 * 2.0**23
 
 Y_BANKS = 2
@@ -34,7 +38,7 @@ SUP_BANKS = 6
 TRANSPOSE_AHEAD = SUP_BANKS - 3
 MIX_AHEAD = TRANSPOSE_AHEAD + N_CHUNKS + 1
 FINISH_BEHIND = ROW_TILES + 1
-VECTOR_GROUPS = 3
+VECTOR_GROUPS = 2
 GPSIMD_TILES = (GROUPS - VECTOR_GROUPS) * ROW_TILES
 
 FLOPS = 2 * ROWS * K * STATES * N
@@ -61,12 +65,13 @@ def tile_quantumsuperposition_t_e_kernel(
         const = ctx.enter_context(tc.tile_pool(name="const", bufs=1))
         small = ctx.enter_context(tc.tile_pool(name="small", bufs=1))
 
+        per_param = STATES * N_CHUNKS
         param_rows = const.tile([P, P], BF16)
         nc.vector.memset(param_rows[:], 0.0)
-        for place, param in enumerate((amplitude_weights, phase_weights, b)):
-            first = place * STATES * N_CHUNKS
+        param_list = (amplitude_weights, phase_weights, b)
+        for place, param in enumerate(param_list):
             nc.sync.dma_start(
-                out=param_rows[first : first + STATES * N_CHUNKS, :],
+                out=param_rows[place * per_param : (place + 1) * per_param, :],
                 in_=param.rearrange("s (j p) -> (s j) p", p=P),
             )
 
@@ -88,15 +93,17 @@ def tile_quantumsuperposition_t_e_kernel(
 
         w_scales = const.tile([P, STATES, N], U8, align_bytes=64)
         nc.vector.memset(w_scales[:].bitcast(I32), 0)
-        for quad in range(4):
+        for quad in range(QUADRANTS):
+            top = quad * (P // QUADRANTS)
+            rows_q = slice(quad * LIVE_ROWS, (quad + 1) * LIVE_ROWS)
             nc.sync.dma_start(
-                out=w_scales[32 * quad : 32 * quad + 4, :, :].bitcast(I32),
-                in_=W_scales[:, 4 * quad : 4 * quad + 4, :].rearrange("g r n -> r g n").bitcast(I32),
+                out=w_scales[top : top + LIVE_ROWS, :, :].bitcast(I32),
+                in_=W_scales[:, rows_q, :].rearrange("s q n -> q s n").bitcast(I32),
             )
         w_codes = const.tile([P, STATES, N], U32, align_bytes=64)
         nc.sync.dma_start(
             out=w_codes[:].bitcast(I32),
-            in_=W_words.rearrange("g p n t -> p g (n t)").bitcast(I32),
+            in_=W_words.rearrange("s p n t -> p s (n t)").bitcast(I32),
         )
         for blk in range(2, BLOCKS):
             load_x(blk)
@@ -114,6 +121,8 @@ def tile_quantumsuperposition_t_e_kernel(
         x_scales = const.tile([P, BLOCKS, BLOCK_ROWS], U8, align_bytes=64)
         mix_col = const.tile([P, STATES, N_CHUNKS], F32)
         shift_col = const.tile([P, STATES, N_CHUNKS], F32)
+        gamma_row = const.tile([P, N], F32)
+        beta_row = const.tile([P, N], F32)
         by_state = [P, STATES, N_CHUNKS]
 
         with ExitStack() as head:
@@ -122,13 +131,15 @@ def tile_quantumsuperposition_t_e_kernel(
 
             param_ps = head_psum.tile([P, P], BF16, bufs=1)
             nc.tensor.transpose(param_ps[:], param_rows[:], ident_bf[:])
-            params = small.tile([P, 3, STATES, N_CHUNKS], F32)
+            params = small.tile([P, len(param_list), STATES, N_CHUNKS], F32)
             nc.vector.tensor_copy(
                 out=params[:].rearrange("p a s j -> p (a s j)"),
-                in_=param_ps[:, 0 : 3 * STATES * N_CHUNKS],
+                in_=param_ps[:, 0 : len(param_list) * per_param],
             )
-            gamma_row = const.tile([P, N], F32)
-            beta_row = const.tile([P, N], F32)
+            amplitude = params[:, 0, :, :]
+            phase = params[:, 1, :, :]
+            bias = params[:, 2, :, :]
+
             for place, spread in enumerate((gamma_row, beta_row)):
                 spread_ps = head_psum.tile([P, N], F32, bufs=2)
                 nc.tensor.matmul(
@@ -136,13 +147,10 @@ def tile_quantumsuperposition_t_e_kernel(
                 )
                 nc.scalar.copy(out=spread[:], in_=spread_ps[:])
 
-            amplitude = params[:, 0, :, :]
-            phase = params[:, 1, :, :]
-            bias = params[:, 2, :, :]
-
             peak = small.tile([P, N_CHUNKS], F32)
             nc.vector.tensor_max(out=peak[:], in0=amplitude[:, 0, :], in1=amplitude[:, 1, :])
-            nc.vector.tensor_max(out=peak[:], in0=peak[:], in1=amplitude[:, 2, :])
+            for s in range(2, STATES):
+                nc.vector.tensor_max(out=peak[:], in0=peak[:], in1=amplitude[:, s, :])
             expo = small.tile(by_state, F32)
             nc.vector.tensor_tensor(
                 out=expo[:],
@@ -172,21 +180,23 @@ def tile_quantumsuperposition_t_e_kernel(
             grouped_tiles = []
 
             def transpose_block(blk):
-                grouped = grouped_pool.tile([P, 4 * BLOCK_ROWS], BF16, align_bytes=64)
+                grouped = grouped_pool.tile([P, PACK * BLOCK_ROWS], BF16, align_bytes=64)
                 grouped_words = grouped[:].bitcast(F32).rearrange(
-                    "q (t r u) -> q t r u", t=ROW_TILES, u=2
+                    "p (t r u) -> p t r u", t=ROW_TILES, u=2
                 )
                 x_words = x_tiles[blk][:].bitcast(F32)
-                for half, copy_out in enumerate((nc.vector.tensor_copy, nc.scalar.copy)):
+                for pair, copy_out in enumerate((nc.vector.tensor_copy, nc.scalar.copy)):
                     x_t = head_psum.tile([P, 2, 2, P], F32)
-                    for t in range(2):
+                    for member in range(2):
                         for u in range(2):
                             nc.tensor.transpose(
-                                x_t[:, t, u, :], x_words[:, 2 * half + t, u:K_WORDS:2], ident_f32[:]
+                                x_t[:, member, u, :],
+                                x_words[:, 2 * pair + member, u:K_WORDS:2],
+                                ident_f32[:],
                             )
                     copy_out(
-                        out=grouped_words[:, 2 * half : 2 * half + 2, :, :],
-                        in_=x_t[:].rearrange("q t u r -> q t r u"),
+                        out=grouped_words[:, 2 * pair : 2 * pair + 2, :, :],
+                        in_=x_t[:].rearrange("p t u r -> p t r u"),
                     )
                 grouped_tiles.append(grouped)
 
@@ -204,7 +214,8 @@ def tile_quantumsuperposition_t_e_kernel(
 
             total = small.tile([P, N_CHUNKS], F32)
             nc.vector.tensor_add(out=total[:], in0=expo[:, 0, :], in1=expo[:, 1, :])
-            nc.vector.tensor_add(out=total[:], in0=total[:], in1=expo[:, 2, :])
+            for s in range(2, STATES):
+                nc.vector.tensor_add(out=total[:], in0=total[:], in1=expo[:, s, :])
             nc.vector.reciprocal(out=total[:], in_=total[:])
             cosine = small.tile(by_state, F32)
             nc.vector.tensor_mul(out=cosine[:], in0=half_sin[:], in1=half_sin[:])
@@ -221,7 +232,7 @@ def tile_quantumsuperposition_t_e_kernel(
 
         y_psum = ctx.enter_context(tc.psum_pool(name="y_psum", bufs=Y_BANKS))
         sup_psum = ctx.enter_context(tc.psum_pool(name="sup_psum", bufs=SUP_BANKS))
-        sup_t_pool = ctx.enter_context(tc.tile_pool(name="sup_t_pool", bufs=4))
+        sup_t_pool = ctx.enter_context(tc.tile_pool(name="sup_t_pool", bufs=3))
         stat_pool = ctx.enter_context(tc.tile_pool(name="stat_pool", bufs=4))
         out_pool = ctx.enter_context(tc.tile_pool(name="out_pool", bufs=5))
         sup_t_of = {}
@@ -266,7 +277,7 @@ def tile_quantumsuperposition_t_e_kernel(
             sup_of[i] = sup
 
         def row_sums(i):
-            halves = stat_pool.tile([P, 6], F32)
+            halves = stat_pool.tile([P, BN_STATS_DIM], F32)
             nc.vector.bn_stats(out=halves[:], in_=sup_of[i][:])
             halves_of[i] = halves
 

@@ -61,7 +61,6 @@ def tile_quantumsuperposition_t_e_kernel(
     out_groups = out.rearrange("(blk p t) s n -> blk s p t n", p=P, t=ROW_TILES)
 
     with ExitStack() as ctx:
-        ctx.enter_context(tc.manual_schedule())
         const = ctx.enter_context(tc.tile_pool(name="const", bufs=1))
         small = ctx.enter_context(tc.tile_pool(name="small", bufs=1))
 

@@ -41,6 +41,12 @@ FINISH_BEHIND = ROW_TILES + 1
 VECTOR_GROUPS = 2
 GPSIMD_TILES = (GROUPS - VECTOR_GROUPS) * ROW_TILES
 
+FINE_GROUPS = (0, GROUPS - VECTOR_GROUPS - 1)
+FINE_BEHIND = 3
+CHUNKS_IN_BLOCK = STATES * N_CHUNKS
+PREPARE_AT = (1, 3, 6)
+EARLY_BLOCKS = 4
+
 FLOPS = 2 * ROWS * K * STATES * N
 
 
@@ -74,11 +80,6 @@ def tile_quantumsuperposition_t_e_kernel(
                 in_=param.rearrange("s (j p) -> (s j) p", p=P),
             )
 
-        norm_rows = const.tile([P, 2, N], BF16)
-        nc.vector.memset(norm_rows[:], 0.0)
-        nc.sync.dma_start(out=norm_rows[0:1, 0, :], in_=ln_gamma.unsqueeze(0))
-        nc.sync.dma_start(out=norm_rows[0:1, 1, :], in_=ln_beta.unsqueeze(0))
-
         x_pool = ctx.enter_context(tc.tile_pool(name="x_pool", bufs=BLOCKS))
         x_tiles = []
 
@@ -88,7 +89,6 @@ def tile_quantumsuperposition_t_e_kernel(
             x_tiles.append(x_rows)
 
         load_x(0)
-        load_x(1)
 
         w_scales = const.tile([P, STATES, N], U8, align_bytes=64)
         nc.vector.memset(w_scales[:].bitcast(I32), 0)
@@ -100,11 +100,17 @@ def tile_quantumsuperposition_t_e_kernel(
                 in_=W_scales[:, rows_q, :].rearrange("s q n -> q s n").bitcast(I32),
             )
         w_codes = const.tile([P, STATES, N], U32, align_bytes=64)
-        nc.sync.dma_start(
-            out=w_codes[:].bitcast(I32),
-            in_=W_words.rearrange("s p n t -> p s (n t)").bitcast(I32),
-        )
-        for blk in range(2, BLOCKS):
+        for s in range(STATES):
+            nc.sync.dma_start(
+                out=w_codes[:, s, :].bitcast(I32),
+                in_=W_words[s].rearrange("p n t -> p (n t)").bitcast(I32),
+            )
+
+        norm_rows = const.tile([P, 2, N], BF16)
+        nc.vector.memset(norm_rows[:], 0.0)
+        nc.sync.dma_start(out=norm_rows[0:1, 0, :], in_=ln_gamma.unsqueeze(0))
+        nc.sync.dma_start(out=norm_rows[0:1, 1, :], in_=ln_beta.unsqueeze(0))
+        for blk in range(1, BLOCKS):
             load_x(blk)
 
         ident_bf = const.tile([P, P], BF16)
@@ -124,113 +130,111 @@ def tile_quantumsuperposition_t_e_kernel(
         beta_row = const.tile([P, N], F32)
         by_state = [P, STATES, N_CHUNKS]
 
-        with ExitStack() as head:
-            head_psum = head.enter_context(tc.psum_pool(name="head_psum", bufs=4))
-            grouped_pool = head.enter_context(tc.tile_pool(name="grouped_pool", bufs=3))
-
-            param_ps = head_psum.tile([P, P], BF16, bufs=1)
-            nc.tensor.transpose(param_ps[:], param_rows[:], ident_bf[:])
-            params = small.tile([P, len(param_list), STATES, N_CHUNKS], F32)
-            nc.vector.tensor_copy(
-                out=params[:].rearrange("p a s j -> p (a s j)"),
-                in_=param_ps[:, 0 : len(param_list) * per_param],
-            )
-            amplitude = params[:, 0, :, :]
-            phase = params[:, 1, :, :]
-            bias = params[:, 2, :, :]
-
-            for place, spread in enumerate((gamma_row, beta_row)):
-                spread_ps = head_psum.tile([P, N], F32, bufs=2)
-                nc.tensor.matmul(
-                    out=spread_ps[:], lhsT=ones[:], rhs=norm_rows[:, place, :], start=True, stop=True
-                )
-                nc.scalar.copy(out=spread[:], in_=spread_ps[:])
-
-            peak = small.tile([P, N_CHUNKS], F32)
-            nc.vector.tensor_max(out=peak[:], in0=amplitude[:, 0, :], in1=amplitude[:, 1, :])
-            for s in range(2, STATES):
-                nc.vector.tensor_max(out=peak[:], in0=peak[:], in1=amplitude[:, s, :])
-            expo = small.tile(by_state, F32)
-            nc.vector.tensor_tensor(
-                out=expo[:],
-                in0=amplitude,
-                in1=peak[:].unsqueeze(1).to_broadcast(by_state),
-                op=ALU.subtract,
-            )
-            nc.scalar.activation(out=expo[:], in_=expo[:], func=ACT.Exp)
-
-            turns = small.tile(by_state, F32)
-            nc.vector.tensor_scalar(
-                out=turns[:], in0=phase, scalar1=1.0 / (2.0 * math.pi), scalar2=None, op0=ALU.mult
-            )
-            whole = small.tile(by_state, F32)
-            nc.vector.tensor_scalar(
-                out=whole[:], in0=turns[:], scalar1=ROUND_MAGIC, scalar2=None, op0=ALU.add
-            )
-            nc.vector.tensor_scalar(
-                out=whole[:], in0=whole[:], scalar1=ROUND_MAGIC, scalar2=None, op0=ALU.subtract
-            )
-            half_sin = small.tile(by_state, F32)
-            nc.vector.tensor_tensor(out=half_sin[:], in0=turns[:], in1=whole[:], op=ALU.subtract)
-            nc.scalar.activation(out=half_sin[:], in_=half_sin[:], func=ACT.Sin, scale=math.pi)
-            warm = small.tile([P, 1], F32)
-            nc.scalar.activation(out=warm[:], in_=eps[:], func=ACT.Abs_reciprocal_sqrt)
-
-            grouped_tiles = []
-
-            def transpose_block(blk):
-                grouped = grouped_pool.tile([P, PACK * BLOCK_ROWS], BF16, align_bytes=64)
-                grouped_words = grouped[:].bitcast(F32).rearrange(
-                    "p (t r u) -> p t r u", t=ROW_TILES, u=2
-                )
-                x_words = x_tiles[blk][:].bitcast(F32)
-                for pair, copy_out in enumerate((nc.vector.tensor_copy, nc.scalar.copy)):
-                    x_t = head_psum.tile([P, 2, 2, P], F32)
-                    for member in range(2):
-                        for u in range(2):
-                            nc.tensor.transpose(
-                                x_t[:, member, u, :],
-                                x_words[:, 2 * pair + member, u:K_WORDS:2],
-                                ident_f32[:],
-                            )
-                    copy_out(
-                        out=grouped_words[:, 2 * pair : 2 * pair + 2, :, :],
-                        in_=x_t[:].rearrange("p t u r -> p t r u"),
-                    )
-                grouped_tiles.append(grouped)
-
-            def quantise_block(blk):
-                nc.vector.quantize_mx(
-                    out=x_codes[:, blk, :].bitcast(FP8X4),
-                    scales=x_scales[:, blk, :],
-                    in_=grouped_tiles[blk][:],
-                )
-
-            transpose_block(0)
-            for blk in range(1, BLOCKS):
-                transpose_block(blk)
-                quantise_block(blk - 1)
-
-            total = small.tile([P, N_CHUNKS], F32)
-            nc.vector.tensor_add(out=total[:], in0=expo[:, 0, :], in1=expo[:, 1, :])
-            for s in range(2, STATES):
-                nc.vector.tensor_add(out=total[:], in0=total[:], in1=expo[:, s, :])
-            nc.vector.reciprocal(out=total[:], in_=total[:])
-            cosine = small.tile(by_state, F32)
-            nc.vector.tensor_mul(out=cosine[:], in0=half_sin[:], in1=half_sin[:])
-            nc.vector.tensor_scalar(
-                out=cosine[:], in0=cosine[:], scalar1=-2.0, scalar2=1.0, op0=ALU.mult, op1=ALU.add
-            )
-            nc.vector.tensor_mul(
-                out=mix_col[:], in0=expo[:], in1=total[:].unsqueeze(1).to_broadcast(by_state)
-            )
-            nc.vector.tensor_mul(out=mix_col[:], in0=mix_col[:], in1=cosine[:])
-            nc.vector.tensor_mul(out=shift_col[:], in0=bias, in1=mix_col[:])
-
-            quantise_block(BLOCKS - 1)
-
         y_psum = ctx.enter_context(tc.psum_pool(name="y_psum", bufs=Y_BANKS))
-        sup_psum = ctx.enter_context(tc.psum_pool(name="sup_psum", bufs=SUP_BANKS))
+        bank_psum = ctx.enter_context(tc.psum_pool(name="bank_psum", bufs=SUP_BANKS))
+        grouped_pool = ctx.enter_context(tc.tile_pool(name="grouped_pool", bufs=3))
+
+        warm = small.tile([P, 1], F32)
+        nc.scalar.activation(out=warm[:], in_=eps[:], func=ACT.Exp)
+
+        param_ps = bank_psum.tile([P, P], BF16, tag="bank")
+        nc.tensor.transpose(param_ps[:], param_rows[:], ident_bf[:])
+        params = small.tile([P, len(param_list), STATES, N_CHUNKS], F32)
+        nc.vector.tensor_copy(
+            out=params[:].rearrange("p a s j -> p (a s j)"),
+            in_=param_ps[:, 0 : len(param_list) * per_param],
+        )
+        amplitude = params[:, 0, :, :]
+        phase = params[:, 1, :, :]
+        bias = params[:, 2, :, :]
+
+        peak = small.tile([P, N_CHUNKS], F32)
+        nc.vector.tensor_max(out=peak[:], in0=amplitude[:, 0, :], in1=amplitude[:, 1, :])
+        for s in range(2, STATES):
+            nc.vector.tensor_max(out=peak[:], in0=peak[:], in1=amplitude[:, s, :])
+        expo = small.tile(by_state, F32)
+        nc.vector.tensor_tensor(
+            out=expo[:],
+            in0=amplitude,
+            in1=peak[:].unsqueeze(1).to_broadcast(by_state),
+            op=ALU.subtract,
+        )
+        nc.scalar.activation(out=expo[:], in_=expo[:], func=ACT.Exp)
+
+        turns = small.tile(by_state, F32)
+        nc.vector.tensor_scalar(
+            out=turns[:], in0=phase, scalar1=1.0 / (2.0 * math.pi), scalar2=None, op0=ALU.mult
+        )
+        whole = small.tile(by_state, F32)
+        nc.vector.tensor_scalar(
+            out=whole[:], in0=turns[:], scalar1=ROUND_MAGIC, scalar2=None, op0=ALU.add
+        )
+        nc.vector.tensor_scalar(
+            out=whole[:], in0=whole[:], scalar1=ROUND_MAGIC, scalar2=None, op0=ALU.subtract
+        )
+        half_sin = small.tile(by_state, F32)
+        nc.vector.tensor_tensor(out=half_sin[:], in0=turns[:], in1=whole[:], op=ALU.subtract)
+        nc.scalar.activation(out=half_sin[:], in_=half_sin[:], func=ACT.Sin, scale=math.pi)
+        nc.scalar.activation(out=warm[:], in_=eps[:], func=ACT.Abs_reciprocal_sqrt)
+
+        grouped_of = {}
+
+        def transpose_half(blk, pair, copy_out):
+            if pair == 0:
+                grouped = grouped_pool.tile([P, PACK * BLOCK_ROWS], BF16, align_bytes=64)
+                grouped_of[blk] = grouped
+            grouped_words = grouped_of[blk][:].bitcast(F32).rearrange(
+                "p (t r u) -> p t r u", t=ROW_TILES, u=2
+            )
+            x_words = x_tiles[blk][:].bitcast(F32)
+            x_t = bank_psum.tile([P, 2, 2, P], F32, tag="bank")
+            for member in range(2):
+                for u in range(2):
+                    nc.tensor.transpose(
+                        x_t[:, member, u, :],
+                        x_words[:, 2 * pair + member, u:K_WORDS:2],
+                        ident_f32[:],
+                    )
+            copy_out(
+                out=grouped_words[:, 2 * pair : 2 * pair + 2, :, :],
+                in_=x_t[:].rearrange("p t u r -> p t r u"),
+            )
+
+        def quantise_block(blk):
+            nc.vector.quantize_mx(
+                out=x_codes[:, blk, :].bitcast(FP8X4),
+                scales=x_scales[:, blk, :],
+                in_=grouped_of[blk][:],
+            )
+
+        transpose_half(0, 0, nc.vector.tensor_copy)
+        transpose_half(0, 1, nc.vector.tensor_copy)
+
+        total = small.tile([P, N_CHUNKS], F32)
+        nc.vector.tensor_add(out=total[:], in0=expo[:, 0, :], in1=expo[:, 1, :])
+        for s in range(2, STATES):
+            nc.vector.tensor_add(out=total[:], in0=total[:], in1=expo[:, s, :])
+        nc.vector.reciprocal(out=total[:], in_=total[:])
+        cosine = small.tile(by_state, F32)
+        nc.vector.tensor_mul(out=cosine[:], in0=half_sin[:], in1=half_sin[:])
+        nc.vector.tensor_scalar(
+            out=cosine[:], in0=cosine[:], scalar1=-2.0, scalar2=1.0, op0=ALU.mult, op1=ALU.add
+        )
+        nc.vector.tensor_mul(
+            out=mix_col[:], in0=expo[:], in1=total[:].unsqueeze(1).to_broadcast(by_state)
+        )
+        nc.vector.tensor_mul(out=mix_col[:], in0=mix_col[:], in1=cosine[:])
+        nc.vector.tensor_mul(out=shift_col[:], in0=bias, in1=mix_col[:])
+
+        quantise_block(0)
+
+        for place, spread in enumerate((gamma_row, beta_row)):
+            spread_ps = bank_psum.tile([P, N], F32, tag="bank")
+            nc.tensor.matmul(
+                out=spread_ps[:], lhsT=ones[:], rhs=norm_rows[:, place, :], start=True, stop=True
+            )
+            nc.vector.tensor_copy(out=spread[:], in_=spread_ps[:])
+
         sup_t_pool = ctx.enter_context(tc.tile_pool(name="sup_t_pool", bufs=3))
         stat_pool = ctx.enter_context(tc.tile_pool(name="stat_pool", bufs=4))
         out_pool = ctx.enter_context(tc.tile_pool(name="out_pool", bufs=5))
@@ -248,7 +252,7 @@ def tile_quantumsuperposition_t_e_kernel(
                 sup_t = sup_t_pool.tile([P, N_CHUNKS, BLOCK_ROWS], F32)
                 sup_t_of[g] = sup_t
             cols = slice(j * P, (j + 1) * P)
-            y_t = y_psum.tile([P, BLOCK_ROWS], F32)
+            y_t = y_psum.tile([P, BLOCK_ROWS], F32, tag="y_t")
             nc.tensor.matmul_mx(
                 out=y_t[:],
                 lhsT=w_codes[:, s, cols].bitcast(FP8X4),
@@ -268,7 +272,7 @@ def tile_quantumsuperposition_t_e_kernel(
 
         def transpose_tile(i):
             g, t = divmod(i, ROW_TILES)
-            sup = sup_psum.tile([P, N], F32)
+            sup = bank_psum.tile([P, N], F32, tag="bank")
             for j in range(N_CHUNKS):
                 nc.tensor.transpose(
                     sup[:, j * P : (j + 1) * P], sup_t_of[g][:, j, t * P : (t + 1) * P], ident_f32[:]
@@ -286,16 +290,23 @@ def tile_quantumsuperposition_t_e_kernel(
                 mean_var = stat_pool.tile([P, ROW_TILES, 2], F32)
                 mean_var_of[g] = mean_var
             nc.vector.bn_aggr(out=mean_var_of[g][:, t, :], in_=halves_of[i][:])
-            if t == ROW_TILES - 1:
+            if t == 0:
                 rstd = stat_pool.tile([P, ROW_TILES], F32)
+                rstd_of[g] = rstd
+            if g in FINE_GROUPS:
+                done = slice(t, t + 1)
+            elif t == ROW_TILES - 1:
+                done = slice(0, ROW_TILES)
+            else:
+                done = None
+            if done is not None:
                 nc.scalar.activation(
-                    out=rstd[:],
-                    in_=mean_var_of[g][:, :, 1],
+                    out=rstd_of[g][:, done],
+                    in_=mean_var_of[g][:, done, 1],
                     func=ACT.Abs_reciprocal_sqrt,
                     bias=eps[:, 0:1],
                     scale=1.0,
                 )
-                rstd_of[g] = rstd
 
         def centre_times_gamma(i):
             g, t = divmod(i, ROW_TILES)
@@ -316,7 +327,10 @@ def tile_quantumsuperposition_t_e_kernel(
             blk, s = divmod(g, STATES)
             rows = out_of[g][:, t, :]
             nc.scalar.activation(out=rows, in_=rows, func=ACT.Identity, scale=rstd_of[g][:, t : t + 1])
-            if t == ROW_TILES - 1:
+            if g in FINE_GROUPS:
+                nc.gpsimd.tensor_tensor(out=rows, in0=rows, in1=beta_row[:], op=ALU.add)
+                nc.sync.dma_start(out=out_groups[blk, s][:, t, :], in_=rows)
+            elif t == ROW_TILES - 1:
                 nc.gpsimd.tensor_tensor(
                     out=out_of[g][:],
                     in0=out_of[g][:],
@@ -339,9 +353,39 @@ def tile_quantumsuperposition_t_e_kernel(
             )
             nc.sync.dma_start(out=out_groups[blk, s][:, t, :], in_=rows)
 
-        for i in range(-MIX_AHEAD, TILES + 2):
+        prepare_after = {}
+        for blk in range(1, BLOCKS):
+            if blk <= EARLY_BLOCKS:
+                first = 2 * (blk - 1)
+                places = (first, first + 1, first + 2)
+            else:
+                first = (blk - 1) * CHUNKS_IN_BLOCK
+                places = (first + PREPARE_AT[0], first + PREPARE_AT[1], first + PREPARE_AT[2])
+            for what, place in enumerate(places):
+                prepare_after.setdefault(place, []).append((what, blk))
+
+        def prepare_blocks(c):
+            for what, blk in sorted(prepare_after.get(c, [])):
+                if what == 2:
+                    quantise_block(blk)
+                else:
+                    copy_out = nc.vector.tensor_copy if blk <= EARLY_BLOCKS else nc.scalar.copy
+                    transpose_half(blk, what, copy_out)
+
+        beta_bank = None
+        finish_at = {}
+        for tile_no in range(TILES):
+            behind = FINE_BEHIND if tile_no // ROW_TILES in FINE_GROUPS else FINISH_BEHIND
+            finish_at.setdefault(tile_no + behind, []).append(tile_no)
+        for i in range(-MIX_AHEAD, TILES + FINISH_BEHIND):
             if i + MIX_AHEAD < TILES:
                 multiply_and_mix(i + MIX_AHEAD)
+                prepare_blocks(i + MIX_AHEAD)
+            if i + MIX_AHEAD == TILES:
+                beta_bank = y_psum.tile([P, N], F32, tag="y_t")
+                nc.tensor.matmul(
+                    out=beta_bank[:], lhsT=ones[:], rhs=norm_rows[:, 1, :], start=True, stop=True
+                )
             if 0 <= i + TRANSPOSE_AHEAD < TILES:
                 transpose_tile(i + TRANSPOSE_AHEAD)
             if 0 <= i < TILES:
@@ -350,10 +394,8 @@ def tile_quantumsuperposition_t_e_kernel(
                 mean_and_variance(i - 1)
             if 0 <= i - 2 < TILES:
                 centre_times_gamma(i - 2)
-            if 0 <= i - FINISH_BEHIND < GPSIMD_TILES:
-                finish_tile(i - FINISH_BEHIND)
-
-        beta_bank = sup_psum.tile([P, N], F32, tag="sup")
-        nc.tensor.matmul(out=beta_bank[:], lhsT=ones[:], rhs=norm_rows[:, 1, :], start=True, stop=True)
-        for i in range(GPSIMD_TILES, TILES):
-            finish_tile_on_vector(i, beta_bank)
+            for tile_no in finish_at.get(i, []):
+                if tile_no < GPSIMD_TILES:
+                    finish_tile(tile_no)
+                else:
+                    finish_tile_on_vector(tile_no, beta_bank)

@@ -45,7 +45,7 @@ FINE_GROUPS = (0, GROUPS - VECTOR_GROUPS - 1)
 FINE_BEHIND = 3
 CHUNKS_IN_BLOCK = STATES * N_CHUNKS
 PREPARE_AT = (1, 3, 6)
-EARLY_BLOCKS = 4
+EARLY_BLOCKS = 7
 
 FLOPS = 2 * ROWS * K * STATES * N
 
@@ -132,7 +132,7 @@ def tile_quantumsuperposition_t_e_kernel(
 
         y_psum = ctx.enter_context(tc.psum_pool(name="y_psum", bufs=Y_BANKS))
         bank_psum = ctx.enter_context(tc.psum_pool(name="bank_psum", bufs=SUP_BANKS))
-        grouped_pool = ctx.enter_context(tc.tile_pool(name="grouped_pool", bufs=3))
+        grouped_pool = ctx.enter_context(tc.tile_pool(name="grouped_pool", bufs=4))
 
         warm = small.tile([P, 1], F32)
         nc.scalar.activation(out=warm[:], in_=eps[:], func=ACT.Exp)
@@ -356,8 +356,7 @@ def tile_quantumsuperposition_t_e_kernel(
         prepare_after = {}
         for blk in range(1, BLOCKS):
             if blk <= EARLY_BLOCKS:
-                first = 2 * (blk - 1)
-                places = (first, first + 1, first + 2)
+                places = (blk - 1, blk - 1, blk)
             else:
                 first = (blk - 1) * CHUNKS_IN_BLOCK
                 places = (first + PREPARE_AT[0], first + PREPARE_AT[1], first + PREPARE_AT[2])
@@ -369,7 +368,7 @@ def tile_quantumsuperposition_t_e_kernel(
                 if what == 2:
                     quantise_block(blk)
                 else:
-                    copy_out = nc.vector.tensor_copy if blk <= EARLY_BLOCKS else nc.scalar.copy
+                    copy_out = nc.vector.tensor_copy if what == 0 else nc.scalar.copy
                     transpose_half(blk, what, copy_out)
 
         beta_bank = None

@@ -72,7 +72,7 @@ def tile_quantumsuperposition_t_e_kernel(
 
         per_param = STATES * N_CHUNKS
         param_rows = const.tile([P, P], BF16)
-        nc.vector.memset(param_rows[:], 0.0)
+        nc.gpsimd.memset(param_rows[:], 0.0)
         param_list = (amplitude_weights, phase_weights, b)
         for place, param in enumerate(param_list):
             nc.sync.dma_start(
@@ -107,7 +107,7 @@ def tile_quantumsuperposition_t_e_kernel(
             )
 
         norm_rows = const.tile([P, 2, N], BF16)
-        nc.vector.memset(norm_rows[:], 0.0)
+        nc.gpsimd.memset(norm_rows[:], 0.0)
         nc.sync.dma_start(out=norm_rows[0:1, 0, :], in_=ln_gamma.unsqueeze(0))
         nc.sync.dma_start(out=norm_rows[0:1, 1, :], in_=ln_beta.unsqueeze(0))
         for blk in range(1, BLOCKS):
@@ -118,7 +118,7 @@ def tile_quantumsuperposition_t_e_kernel(
         ident_f32 = const.tile([P, P], F32)
         make_identity(nc, ident_f32[:])
         ones = const.tile([P, P], BF16)
-        nc.vector.memset(ones[:], 1.0)
+        nc.gpsimd.memset(ones[:], 1.0)
         eps = const.tile([P, 1], F32)
         nc.vector.memset(eps[:], LN_EPS)
 
@@ -233,7 +233,7 @@ def tile_quantumsuperposition_t_e_kernel(
             nc.tensor.matmul(
                 out=spread_ps[:], lhsT=ones[:], rhs=norm_rows[:, place, :], start=True, stop=True
             )
-            nc.vector.tensor_copy(out=spread[:], in_=spread_ps[:])
+            nc.scalar.copy(out=spread[:], in_=spread_ps[:])
 
         sup_t_pool = ctx.enter_context(tc.tile_pool(name="sup_t_pool", bufs=3))
         stat_pool = ctx.enter_context(tc.tile_pool(name="stat_pool", bufs=4))
@@ -368,8 +368,7 @@ def tile_quantumsuperposition_t_e_kernel(
                 if what == 2:
                     quantise_block(blk)
                 else:
-                    copy_out = nc.vector.tensor_copy if what == 0 else nc.scalar.copy
-                    transpose_half(blk, what, copy_out)
+                    transpose_half(blk, what, nc.scalar.copy)
 
         beta_bank = None
         finish_at = {}

@@ -38,11 +38,13 @@ SUP_BANKS = 6
 TRANSPOSE_AHEAD = SUP_BANKS - 3
 MIX_AHEAD = TRANSPOSE_AHEAD + N_CHUNKS + 1
 FINISH_BEHIND = ROW_TILES + 1
-VECTOR_GROUPS = 2
+VECTOR_GROUPS = 3
 GPSIMD_TILES = (GROUPS - VECTOR_GROUPS) * ROW_TILES
 
-FINE_GROUPS = (0, GROUPS - VECTOR_GROUPS - 1)
+FINE_GROUPS = (0,) + tuple(range(GROUPS - VECTOR_GROUPS - 1, GROUPS))
+SCALAR_STAT_TILES = tuple(range(TILES - 6, TILES))
 FINE_BEHIND = 3
+EARLY_AFTER = N_CHUNKS
 CHUNKS_IN_BLOCK = STATES * N_CHUNKS
 PREPARE_AT = (1, 3, 6)
 EARLY_BLOCKS = 7
@@ -241,6 +243,8 @@ def tile_quantumsuperposition_t_e_kernel(
         sup_t_of = {}
         sup_of = {}
         halves_of = {}
+        neg_mean_of = {}
+        spent_pool = ctx.enter_context(tc.tile_pool(name="spent_pool", bufs=2))
         mean_var_of = {}
         rstd_of = {}
         out_of = {}
@@ -280,19 +284,46 @@ def tile_quantumsuperposition_t_e_kernel(
             sup_of[i] = sup
 
         def row_sums(i):
+            g, t = divmod(i, ROW_TILES)
+            if t == 0:
+                mean_var = stat_pool.tile([P, ROW_TILES, 2], F32)
+                mean_var_of[g] = mean_var
+                rstd = stat_pool.tile([P, ROW_TILES], F32)
+                rstd_of[g] = rstd
+            if i in SCALAR_STAT_TILES:
+                neg_mean = stat_pool.tile([P, 1], F32)
+                spent = spent_pool.tile([P, N], F32)
+                nc.scalar.activation(
+                    out=spent[:], in_=sup_of[i][:], func=ACT.Identity, scale=-1.0 / N, accum_out=neg_mean[:]
+                )
+                neg_mean_of[i] = neg_mean
+                squares = stat_pool.tile([P, 1], F32)
+                spent = spent_pool.tile([P, N], F32)
+                nc.scalar.activation(
+                    out=spent[:],
+                    in_=sup_of[i][:],
+                    func=ACT.Square,
+                    bias=neg_mean[:, 0:1],
+                    scale=1.0,
+                    accum_out=squares[:],
+                )
+                nc.scalar.activation(
+                    out=rstd_of[g][:, t : t + 1],
+                    in_=squares[:],
+                    func=ACT.Abs_reciprocal_sqrt,
+                    bias=eps[:, 0:1],
+                    scale=1.0 / N,
+                )
+                return
             halves = stat_pool.tile([P, BN_STATS_DIM], F32)
             nc.vector.bn_stats(out=halves[:], in_=sup_of[i][:])
             halves_of[i] = halves
 
         def mean_and_variance(i):
             g, t = divmod(i, ROW_TILES)
-            if t == 0:
-                mean_var = stat_pool.tile([P, ROW_TILES, 2], F32)
-                mean_var_of[g] = mean_var
+            if i in SCALAR_STAT_TILES:
+                return
             nc.vector.bn_aggr(out=mean_var_of[g][:, t, :], in_=halves_of[i][:])
-            if t == 0:
-                rstd = stat_pool.tile([P, ROW_TILES], F32)
-                rstd_of[g] = rstd
             if g in FINE_GROUPS:
                 done = slice(t, t + 1)
             elif t == ROW_TILES - 1:
@@ -313,12 +344,16 @@ def tile_quantumsuperposition_t_e_kernel(
             if t == 0:
                 out_tile = out_pool.tile([P, ROW_TILES, N], F32)
                 out_of[g] = out_tile
+            if i in SCALAR_STAT_TILES:
+                centre, centre_op = neg_mean_of[i][:, 0:1], ALU.add
+            else:
+                centre, centre_op = mean_var_of[g][:, t, 0:1], ALU.subtract
             nc.vector.scalar_tensor_tensor(
                 out=out_of[g][:, t, :],
                 in0=sup_of[i][:],
-                scalar=mean_var_of[g][:, t, 0:1],
+                scalar=centre,
                 in1=gamma_row[:],
-                op0=ALU.subtract,
+                op0=centre_op,
                 op1=ALU.mult,
             )
 
@@ -356,7 +391,7 @@ def tile_quantumsuperposition_t_e_kernel(
         prepare_after = {}
         for blk in range(1, BLOCKS):
             if blk <= EARLY_BLOCKS:
-                places = (blk - 1, blk - 1, blk)
+                places = (blk + EARLY_AFTER - 1, blk + EARLY_AFTER - 1, blk + EARLY_AFTER)
             else:
                 first = (blk - 1) * CHUNKS_IN_BLOCK
                 places = (first + PREPARE_AT[0], first + PREPARE_AT[1], first + PREPARE_AT[2])
@@ -374,7 +409,10 @@ def tile_quantumsuperposition_t_e_kernel(
         finish_at = {}
         for tile_no in range(TILES):
             behind = FINE_BEHIND if tile_no // ROW_TILES in FINE_GROUPS else FINISH_BEHIND
-            finish_at.setdefault(tile_no + behind, []).append(tile_no)
+            step = tile_no + behind
+            if tile_no >= GPSIMD_TILES:
+                step = max(step, TILES - MIX_AHEAD)
+            finish_at.setdefault(step, []).append(tile_no)
         for i in range(-MIX_AHEAD, TILES + FINISH_BEHIND):
             if i + MIX_AHEAD < TILES:
                 multiply_and_mix(i + MIX_AHEAD)

@@ -33,12 +33,12 @@ TILES = GROUPS * ROW_TILES
 BN_STATS_DIM = 6
 ROUND_MAGIC = 1.5 * 2.0**23
 
-Y_BANKS = 2
-SUP_BANKS = 6
+Y_BANKS = 3
+SUP_BANKS = 5
 TRANSPOSE_AHEAD = SUP_BANKS - 3
 MIX_AHEAD = TRANSPOSE_AHEAD + N_CHUNKS + 1
 FINISH_BEHIND = ROW_TILES + 1
-VECTOR_GROUPS = 3
+VECTOR_GROUPS = 4
 GPSIMD_TILES = (GROUPS - VECTOR_GROUPS) * ROW_TILES
 
 FINE_GROUPS = (0,) + tuple(range(GROUPS - VECTOR_GROUPS - 1, GROUPS))

import math
from contextlib import ExitStack

import concourse.mybir as mybir
from concourse.masks import make_identity

F32 = mybir.dt.float32
BF16 = mybir.dt.bfloat16
I32 = mybir.dt.int32
U32 = mybir.dt.uint32
U8 = mybir.dt.uint8
FP8X4 = mybir.dt.float8_e4m3fn_x4
ALU = mybir.AluOpType
ACT = mybir.ActivationFunctionType

P = 128
ROWS = 4096
K = 512
STATES = 3
N = 512
LN_EPS = 1e-5

PACK = 4
QUADRANTS = 4
LIVE_ROWS = 4
BLOCK_ROWS = 512
BLOCKS = ROWS // BLOCK_ROWS
ROW_TILES = BLOCK_ROWS // P
N_CHUNKS = N // P
K_WORDS = K // 2
GROUPS = BLOCKS * STATES
TILES = GROUPS * ROW_TILES
BN_STATS_DIM = 6
ROUND_MAGIC = 1.5 * 2.0**23

Y_BANKS = 3
SUP_BANKS = 5
TRANSPOSE_AHEAD = SUP_BANKS - 3
MIX_AHEAD = TRANSPOSE_AHEAD + N_CHUNKS + 1
FINISH_BEHIND = ROW_TILES + 1
VECTOR_GROUPS = 4
GPSIMD_TILES = (GROUPS - VECTOR_GROUPS) * ROW_TILES

FINE_GROUPS = (0,) + tuple(range(GROUPS - VECTOR_GROUPS - 1, GROUPS))
SCALAR_STAT_TILES = tuple(range(TILES - 6, TILES))
FINE_BEHIND = 3
EARLY_AFTER = N_CHUNKS
CHUNKS_IN_BLOCK = STATES * N_CHUNKS
PREPARE_AT = (1, 3, 6)
EARLY_BLOCKS = 7

FLOPS = 2 * ROWS * K * STATES * N


def tile_quantumsuperposition_t_e_kernel(
    tc,
    language_features,
    W_words,
    W_scales,
    b,
    amplitude_weights,
    phase_weights,
    ln_gamma,
    ln_beta,
    out,
):
    nc = tc.nc
    x_blocks = language_features.rearrange("(blk p t) k -> blk p t k", p=P, t=ROW_TILES)
    out_groups = out.rearrange("(blk p t) s n -> blk s p t n", p=P, t=ROW_TILES)

    with ExitStack() as ctx:
        const = ctx.enter_context(tc.tile_pool(name="const", bufs=1))
        small = ctx.enter_context(tc.tile_pool(name="small", bufs=1))

        per_param = STATES * N_CHUNKS
        param_rows = const.tile([P, P], BF16)
        nc.gpsimd.memset(param_rows[:], 0.0)
        param_list = (amplitude_weights, phase_weights, b)
        for place, param in enumerate(param_list):
            nc.sync.dma_start(
                out=param_rows[place * per_param : (place + 1) * per_param, :],
                in_=param.rearrange("s (j p) -> (s j) p", p=P),
            )

        x_pool = ctx.enter_context(tc.tile_pool(name="x_pool", bufs=BLOCKS))
        x_tiles = []

        def load_x(blk):
            x_rows = x_pool.tile([P, ROW_TILES, K], BF16)
            nc.sync.dma_start(out=x_rows[:], in_=x_blocks[blk])
            x_tiles.append(x_rows)

        load_x(0)

        w_scales = const.tile([P, STATES, N], U8, align_bytes=64)
        nc.vector.memset(w_scales[:].bitcast(I32), 0)
        for quad in range(QUADRANTS):
            top = quad * (P // QUADRANTS)
            rows_q = slice(quad * LIVE_ROWS, (quad + 1) * LIVE_ROWS)
            nc.sync.dma_start(
                out=w_scales[top : top + LIVE_ROWS, :, :].bitcast(I32),
                in_=W_scales[:, rows_q, :].rearrange("s q n -> q s n").bitcast(I32),
            )
        w_codes = const.tile([P, STATES, N], U32, align_bytes=64)
        for s in range(STATES):
            nc.sync.dma_start(
                out=w_codes[:, s, :].bitcast(I32),
                in_=W_words[s].rearrange("p n t -> p (n t)").bitcast(I32),
            )

        norm_rows = const.tile([P, 2, N], BF16)
        nc.gpsimd.memset(norm_rows[:], 0.0)
        nc.sync.dma_start(out=norm_rows[0:1, 0, :], in_=ln_gamma.unsqueeze(0))
        nc.sync.dma_start(out=norm_rows[0:1, 1, :], in_=ln_beta.unsqueeze(0))
        for blk in range(1, BLOCKS):
            load_x(blk)

        ident_bf = const.tile([P, P], BF16)
        make_identity(nc, ident_bf[:])
        ident_f32 = const.tile([P, P], F32)
        make_identity(nc, ident_f32[:])
        ones = const.tile([P, P], BF16)
        nc.gpsimd.memset(ones[:], 1.0)
        eps = const.tile([P, 1], F32)
        nc.vector.memset(eps[:], LN_EPS)

        x_codes = const.tile([P, BLOCKS, BLOCK_ROWS], U32, align_bytes=64)
        x_scales = const.tile([P, BLOCKS, BLOCK_ROWS], U8, align_bytes=64)
        mix_col = const.tile([P, STATES, N_CHUNKS], F32)
        shift_col = const.tile([P, STATES, N_CHUNKS], F32)
        gamma_row = const.tile([P, N], F32)
        beta_row = const.tile([P, N], F32)
        by_state = [P, STATES, N_CHUNKS]

        y_psum = ctx.enter_context(tc.psum_pool(name="y_psum", bufs=Y_BANKS))
        bank_psum = ctx.enter_context(tc.psum_pool(name="bank_psum", bufs=SUP_BANKS))
        grouped_pool = ctx.enter_context(tc.tile_pool(name="grouped_pool", bufs=4))

        warm = small.tile([P, 1], F32)
        nc.scalar.activation(out=warm[:], in_=eps[:], func=ACT.Exp)

        param_ps = bank_psum.tile([P, P], BF16, tag="bank")
        nc.tensor.transpose(param_ps[:], param_rows[:], ident_bf[:])
        params = small.tile([P, len(param_list), STATES, N_CHUNKS], F32)
        nc.vector.tensor_copy(
            out=params[:].rearrange("p a s j -> p (a s j)"),
            in_=param_ps[:, 0 : len(param_list) * per_param],
        )
        amplitude = params[:, 0, :, :]
        phase = params[:, 1, :, :]
        bias = params[:, 2, :, :]

        peak = small.tile([P, N_CHUNKS], F32)
        nc.vector.tensor_max(out=peak[:], in0=amplitude[:, 0, :], in1=amplitude[:, 1, :])
        for s in range(2, STATES):
            nc.vector.tensor_max(out=peak[:], in0=peak[:], in1=amplitude[:, s, :])
        expo = small.tile(by_state, F32)
        nc.vector.tensor_tensor(
            out=expo[:],
            in0=amplitude,
            in1=peak[:].unsqueeze(1).to_broadcast(by_state),
            op=ALU.subtract,
        )
        nc.scalar.activation(out=expo[:], in_=expo[:], func=ACT.Exp)

        turns = small.tile(by_state, F32)
        nc.vector.tensor_scalar(
            out=turns[:], in0=phase, scalar1=1.0 / (2.0 * math.pi), scalar2=None, op0=ALU.mult
        )
        whole = small.tile(by_state, F32)
        nc.vector.tensor_scalar(
            out=whole[:], in0=turns[:], scalar1=ROUND_MAGIC, scalar2=None, op0=ALU.add
        )
        nc.vector.tensor_scalar(
            out=whole[:], in0=whole[:], scalar1=ROUND_MAGIC, scalar2=None, op0=ALU.subtract
        )
        half_sin = small.tile(by_state, F32)
        nc.vector.tensor_tensor(out=half_sin[:], in0=turns[:], in1=whole[:], op=ALU.subtract)
        nc.scalar.activation(out=half_sin[:], in_=half_sin[:], func=ACT.Sin, scale=math.pi)
        nc.scalar.activation(out=warm[:], in_=eps[:], func=ACT.Abs_reciprocal_sqrt)

        grouped_of = {}

        def transpose_half(blk, pair, copy_out):
            if pair == 0:
                grouped = grouped_pool.tile([P, PACK * BLOCK_ROWS], BF16, align_bytes=64)
                grouped_of[blk] = grouped
            grouped_words = grouped_of[blk][:].bitcast(F32).rearrange(
                "p (t r u) -> p t r u", t=ROW_TILES, u=2
            )
            x_words = x_tiles[blk][:].bitcast(F32)
            x_t = bank_psum.tile([P, 2, 2, P], F32, tag="bank")
            for member in range(2):
                for u in range(2):
                    nc.tensor.transpose(
                        x_t[:, member, u, :],
                        x_words[:, 2 * pair + member, u:K_WORDS:2],
                        ident_f32[:],
                    )
            copy_out(
                out=grouped_words[:, 2 * pair : 2 * pair + 2, :, :],
                in_=x_t[:].rearrange("p t u r -> p t r u"),
            )

        def quantise_block(blk):
            nc.vector.quantize_mx(
                out=x_codes[:, blk, :].bitcast(FP8X4),
                scales=x_scales[:, blk, :],
                in_=grouped_of[blk][:],
            )

        transpose_half(0, 0, nc.vector.tensor_copy)
        transpose_half(0, 1, nc.vector.tensor_copy)

        total = small.tile([P, N_CHUNKS], F32)
        nc.vector.tensor_add(out=total[:], in0=expo[:, 0, :], in1=expo[:, 1, :])
        for s in range(2, STATES):
            nc.vector.tensor_add(out=total[:], in0=total[:], in1=expo[:, s, :])
        nc.vector.reciprocal(out=total[:], in_=total[:])
        cosine = small.tile(by_state, F32)
        nc.vector.tensor_mul(out=cosine[:], in0=half_sin[:], in1=half_sin[:])
        nc.vector.tensor_scalar(
            out=cosine[:], in0=cosine[:], scalar1=-2.0, scalar2=1.0, op0=ALU.mult, op1=ALU.add
        )
        nc.vector.tensor_mul(
            out=mix_col[:], in0=expo[:], in1=total[:].unsqueeze(1).to_broadcast(by_state)
        )
        nc.vector.tensor_mul(out=mix_col[:], in0=mix_col[:], in1=cosine[:])
        nc.vector.tensor_mul(out=shift_col[:], in0=bias, in1=mix_col[:])

        quantise_block(0)

        for place, spread in enumerate((gamma_row, beta_row)):
            spread_ps = bank_psum.tile([P, N], F32, tag="bank")
            nc.tensor.matmul(
                out=spread_ps[:], lhsT=ones[:], rhs=norm_rows[:, place, :], start=True, stop=True
            )
            nc.scalar.copy(out=spread[:], in_=spread_ps[:])

        sup_t_pool = ctx.enter_context(tc.tile_pool(name="sup_t_pool", bufs=3))
        stat_pool = ctx.enter_context(tc.tile_pool(name="stat_pool", bufs=4))
        out_pool = ctx.enter_context(tc.tile_pool(name="out_pool", bufs=5))
        sup_t_of = {}
        sup_of = {}
        halves_of = {}
        neg_mean_of = {}
        spent_pool = ctx.enter_context(tc.tile_pool(name="spent_pool", bufs=2))
        mean_var_of = {}
        rstd_of = {}
        out_of = {}

        def multiply_and_mix(c):
            g, j = divmod(c, N_CHUNKS)
            blk, s = divmod(g, STATES)
            if j == 0:
                sup_t = sup_t_pool.tile([P, N_CHUNKS, BLOCK_ROWS], F32)
                sup_t_of[g] = sup_t
            cols = slice(j * P, (j + 1) * P)
            y_t = y_psum.tile([P, BLOCK_ROWS], F32, tag="y_t")
            nc.tensor.matmul_mx(
                out=y_t[:],
                lhsT=w_codes[:, s, cols].bitcast(FP8X4),
                lhsT_scale=w_scales[:, s, cols],
                rhs=x_codes[:, blk, :].bitcast(FP8X4),
                rhs_scale=x_scales[:, blk, :],
                start=True,
                stop=True,
            )
            nc.scalar.activation(
                out=sup_t_of[g][:, j, :],
                in_=y_t[:],
                func=ACT.Identity,
                scale=mix_col[:, s, j : j + 1],
                bias=shift_col[:, s, j : j + 1],
            )

        def transpose_tile(i):
            g, t = divmod(i, ROW_TILES)
            sup = bank_psum.tile([P, N], F32, tag="bank")
            for j in range(N_CHUNKS):
                nc.tensor.transpose(
                    sup[:, j * P : (j + 1) * P], sup_t_of[g][:, j, t * P : (t + 1) * P], ident_f32[:]
                )
            sup_of[i] = sup

        def row_sums(i):
            g, t = divmod(i, ROW_TILES)
            if t == 0:
                mean_var = stat_pool.tile([P, ROW_TILES, 2], F32)
                mean_var_of[g] = mean_var
                rstd = stat_pool.tile([P, ROW_TILES], F32)
                rstd_of[g] = rstd
            if i in SCALAR_STAT_TILES:
                neg_mean = stat_pool.tile([P, 1], F32)
                spent = spent_pool.tile([P, N], F32)
                nc.scalar.activation(
                    out=spent[:], in_=sup_of[i][:], func=ACT.Identity, scale=-1.0 / N, accum_out=neg_mean[:]
                )
                neg_mean_of[i] = neg_mean
                squares = stat_pool.tile([P, 1], F32)
                spent = spent_pool.tile([P, N], F32)
                nc.scalar.activation(
                    out=spent[:],
                    in_=sup_of[i][:],
                    func=ACT.Square,
                    bias=neg_mean[:, 0:1],
                    scale=1.0,
                    accum_out=squares[:],
                )
                nc.scalar.activation(
                    out=rstd_of[g][:, t : t + 1],
                    in_=squares[:],
                    func=ACT.Abs_reciprocal_sqrt,
                    bias=eps[:, 0:1],
                    scale=1.0 / N,
                )
                return
            halves = stat_pool.tile([P, BN_STATS_DIM], F32)
            nc.vector.bn_stats(out=halves[:], in_=sup_of[i][:])
            halves_of[i] = halves

        def mean_and_variance(i):
            g, t = divmod(i, ROW_TILES)
            if i in SCALAR_STAT_TILES:
                return
            nc.vector.bn_aggr(out=mean_var_of[g][:, t, :], in_=halves_of[i][:])
            if g in FINE_GROUPS:
                done = slice(t, t + 1)
            elif t == ROW_TILES - 1:
                done = slice(0, ROW_TILES)
            else:
                done = None
            if done is not None:
                nc.scalar.activation(
                    out=rstd_of[g][:, done],
                    in_=mean_var_of[g][:, done, 1],
                    func=ACT.Abs_reciprocal_sqrt,
                    bias=eps[:, 0:1],
                    scale=1.0,
                )

        def centre_times_gamma(i):
            g, t = divmod(i, ROW_TILES)
            if t == 0:
                out_tile = out_pool.tile([P, ROW_TILES, N], F32)
                out_of[g] = out_tile
            if i in SCALAR_STAT_TILES:
                centre, centre_op = neg_mean_of[i][:, 0:1], ALU.add
            else:
                centre, centre_op = mean_var_of[g][:, t, 0:1], ALU.subtract
            nc.vector.scalar_tensor_tensor(
                out=out_of[g][:, t, :],
                in0=sup_of[i][:],
                scalar=centre,
                in1=gamma_row[:],
                op0=centre_op,
                op1=ALU.mult,
            )

        def finish_tile(i):
            g, t = divmod(i, ROW_TILES)
            blk, s = divmod(g, STATES)
            rows = out_of[g][:, t, :]
            nc.scalar.activation(out=rows, in_=rows, func=ACT.Identity, scale=rstd_of[g][:, t : t + 1])
            if g in FINE_GROUPS:
                nc.gpsimd.tensor_tensor(out=rows, in0=rows, in1=beta_row[:], op=ALU.add)
                nc.sync.dma_start(out=out_groups[blk, s][:, t, :], in_=rows)
            elif t == ROW_TILES - 1:
                nc.gpsimd.tensor_tensor(
                    out=out_of[g][:],
                    in0=out_of[g][:],
                    in1=beta_row[:].unsqueeze(1).to_broadcast([P, ROW_TILES, N]),
                    op=ALU.add,
                )
                nc.sync.dma_start(out=out_groups[blk, s], in_=out_of[g][:])

        def finish_tile_on_vector(i, beta_bank):
            g, t = divmod(i, ROW_TILES)
            blk, s = divmod(g, STATES)
            rows = out_of[g][:, t, :]
            nc.vector.scalar_tensor_tensor(
                out=rows,
                in0=rows,
                scalar=rstd_of[g][:, t : t + 1],
                in1=beta_bank[:],
                op0=ALU.mult,
                op1=ALU.add,
            )
            nc.sync.dma_start(out=out_groups[blk, s][:, t, :], in_=rows)

        prepare_after = {}
        for blk in range(1, BLOCKS):
            if blk <= EARLY_BLOCKS:
                places = (blk + EARLY_AFTER - 1, blk + EARLY_AFTER - 1, blk + EARLY_AFTER)
            else:
                first = (blk - 1) * CHUNKS_IN_BLOCK
                places = (first + PREPARE_AT[0], first + PREPARE_AT[1], first + PREPARE_AT[2])
            for what, place in enumerate(places):
                prepare_after.setdefault(place, []).append((what, blk))

        def prepare_blocks(c):
            for what, blk in sorted(prepare_after.get(c, [])):
                if what == 2:
                    quantise_block(blk)
                else:
                    transpose_half(blk, what, nc.scalar.copy)

        beta_bank = None
        finish_at = {}
        for tile_no in range(TILES):
            behind = FINE_BEHIND if tile_no // ROW_TILES in FINE_GROUPS else FINISH_BEHIND
            step = tile_no + behind
            if tile_no >= GPSIMD_TILES:
                step = max(step, TILES - MIX_AHEAD)
            finish_at.setdefault(step, []).append(tile_no)
        for i in range(-MIX_AHEAD, TILES + FINISH_BEHIND):
            if i + MIX_AHEAD < TILES:
                multiply_and_mix(i + MIX_AHEAD)
                prepare_blocks(i + MIX_AHEAD)
            if i + MIX_AHEAD == TILES:
                beta_bank = y_psum.tile([P, N], F32, tag="y_t")
                nc.tensor.matmul(
                    out=beta_bank[:], lhsT=ones[:], rhs=norm_rows[:, 1, :], start=True, stop=True
                )
            if 0 <= i + TRANSPOSE_AHEAD < TILES:
                transpose_tile(i + TRANSPOSE_AHEAD)
            if 0 <= i < TILES:
                row_sums(i)
            if 0 <= i - 1 < TILES:
                mean_and_variance(i - 1)
            if 0 <= i - 2 < TILES:
                centre_times_gamma(i - 2)
            for tile_no in finish_at.get(i, []):
                if tile_no < GPSIMD_TILES:
                    finish_tile(tile_no)
                else:
                    finish_tile_on_vector(tile_no, beta_bank)
